import numpy as np
import ml_dtypes


def mxq(x, axis, fmt="e4m3"):
    dtype, down = {"e4m3": (ml_dtypes.float8_e4m3fn, 7), "e5m2": (ml_dtypes.float8_e5m2, 14)}[fmt]
    v = np.moveaxis(np.asarray(x, np.float32).astype(ml_dtypes.bfloat16).astype(np.float64), axis, -1)
    blocks = v.reshape(v.shape[:-1] + (-1, 32))
    amax = np.abs(blocks).max(-1, keepdims=True)
    byte = np.maximum(np.where(amax > 0, np.frexp(amax)[1] - 1 + 127, 0) - down, 1)
    scale = np.exp2(byte - 127.0)
    codes = (blocks / scale).astype(np.float32).astype(dtype).astype(np.float64)
    return np.moveaxis((codes * scale).reshape(v.shape), -1, axis)


WIDE = False


def mx_kscale(k):
    if not WIDE:
        return np.ones(k)
    levels = np.array([10, -10, 5, -5, 0])
    a = np.random.permutation(np.resize(levels, k // 512 * 4)).reshape(k // 512, 4)
    idx = np.arange(k)
    return np.exp2(a[idx // 512, idx % 128 // 32])


BF16 = ml_dtypes.bfloat16


def bf(x):
    return np.asarray(x, np.float32).astype(BF16)


def f64(x):
    return np.asarray(x).astype(np.float64)


B, S, E, HID, H = 2, 128, 512, 1024, 8
DH = HID // H


def setup_inputs():
    t = mx_kscale(HID)
    kv_rms = np.hypot(6.0 * np.sqrt(S), 0.19 * S)
    return {"q_feat": bf(1.0 + 2.8 * np.random.standard_normal((B, H, S, DH))),
            "kv": bf(np.random.standard_normal((B, H, DH, DH)) * kv_rms * t.reshape(H, 1, DH)),
            "denom": bf(S * DH * (1.0 + 0.1 * np.random.standard_normal((B, H, 1, 1)))),
            "Wo": bf(np.random.standard_normal((HID, E)) * 4.0 / np.sqrt(HID) / t[:, None]),
            "bo": bf(np.random.standard_normal(E) * 0.1)}


def reference(q_feat, kv, denom, Wo, bo):
    qkv = f64(q_feat) @ f64(kv)
    ctx = qkv / f64(denom)
    ctx = ctx.transpose(0, 2, 1, 3).reshape(B, S, HID)
    return (mxq(ctx, 2, "e4m3") @ mxq(f64(Wo), 0, "e4m3")) + f64(bo)

@@ -1,0 +1,162 @@
+from contextlib import ExitStack
+
+import concourse.mybir as mybir
+from concourse.masks import make_identity
+
+BF16 = mybir.dt.bfloat16
+F32 = mybir.dt.float32
+U32 = mybir.dt.uint32
+U8 = mybir.dt.uint8
+FP8X4 = mybir.dt.float8_e4m3fn_x4
+MULT = mybir.AluOpType.mult
+ADD = mybir.AluOpType.add
+
+P = 128
+B = 2
+H = 8
+S = 128
+DH = 128
+E = 512
+PACK = 4
+PASSES = H // PACK
+ROWS = 8
+RUNS = S // ROWS
+HALF = ROWS // 2
+BIAS_ROWS = E // P
+VECTOR_COLS = 256
+
+FLOPS = 2 * B * H * S * DH * DH + 2 * B * S * H * DH * E
+
+
+def tile_linearattention_pb_s_kernel(tc, q_feat, kv, denom, Wo, bo, out):
+    nc = tc.nc
+    with ExitStack() as ctx:
+        keep = ctx.enter_context(tc.tile_pool(name="keep", bufs=1))
+        psum_t = ctx.enter_context(tc.psum_pool(name="psum_t", bufs=2))
+        psum_c = ctx.enter_context(tc.psum_pool(name="psum_c", bufs=4))
+        psum_o = ctx.enter_context(tc.psum_pool(name="psum_o", bufs=2))
+
+        q_rows = []
+        for b in range(B):
+            q_b = keep.tile([P, ROWS, DH], BF16, name="q_rows%d" % b)
+            nc.sync.dma_start(out=q_b[:], in_=q_feat[b].rearrange("h (u j) d -> (h u) j d", j=ROWS))
+            q_rows.append(q_b)
+        kv_sb = []
+        for b in range(B):
+            kv_b = keep.tile([P, H, DH], BF16, name="kv_sb%d" % b)
+            nc.sync.dma_start(out=kv_b[:], in_=kv[b].rearrange("h d e -> d h e"))
+            kv_sb.append(kv_b)
+        wo_view = Wo.rearrange("(g t p) n -> g p t n", t=PACK, p=P)
+        wo_raw = []
+        for g in range(PASSES):
+            wo_g = keep.tile([P, PACK, E], BF16, name="wo_raw%d" % g)
+            nc.sync.dma_start(out=wo_g[:], in_=wo_view[g])
+            wo_raw.append(wo_g)
+
+        vec_rows = keep.tile([P, P], BF16, name="vec_rows")
+        nc.vector.memset(vec_rows[:], 0.0)
+        nc.scalar.dma_start(out=vec_rows[0:BIAS_ROWS, :], in_=bo.rearrange("(c n) -> c n", c=BIAS_ROWS))
+        nc.scalar.dma_start(
+            out=vec_rows[BIAS_ROWS : BIAS_ROWS + 1, 0 : B * H],
+            in_=denom.rearrange("b h x y -> (x y) (b h)"),
+        )
+
+        ident = keep.tile([P, P], BF16, name="ident")
+        make_identity(nc, ident[:])
+
+        q_t = []
+        for b in range(B):
+            q_t_b = keep.tile([P, H, ROWS, RUNS], BF16, name="q_t%d" % b)
+            for half in range(2):
+                t_ps = psum_t.tile([P, HALF, P], BF16, name="t_ps")
+                for jj in range(HALF):
+                    nc.tensor.transpose(t_ps[:, jj, :], q_rows[b][:, half * HALF + jj, :], ident[:])
+                sorted_view = t_ps[:].rearrange("d j (h u) -> d h j u", u=RUNS)
+                target = q_t_b[:, :, half * HALF : (half + 1) * HALF, :]
+                if half == 0:
+                    nc.vector.tensor_copy(out=target, in_=sorted_view)
+                else:
+                    nc.scalar.copy(out=target, in_=sorted_view)
+            q_t.append(q_t_b)
+
+        cols_ps = psum_o.tile([P, P], BF16, name="o_ps")
+        nc.tensor.transpose(cols_ps[:], vec_rows[:], ident[:])
+        vec_cols = keep.tile([P, BIAS_ROWS + 1], BF16, name="vec_cols")
+        nc.vector.tensor_copy(out=vec_cols[:], in_=cols_ps[:, 0 : BIAS_ROWS + 1])
+        spread_ps = psum_o.tile([P, BIAS_ROWS + 1, P], BF16, name="o_ps")
+        for c in range(BIAS_ROWS + 1):
+            nc.tensor.transpose(spread_ps[:, c, :], vec_cols[:, c : c + 1].to_broadcast([P, P]), ident[:])
+        recip = keep.tile([P, B * H], F32, name="recip")
+        nc.vector.reciprocal(out=recip[:], in_=spread_ps[:, BIAS_ROWS, 0 : B * H])
+        bias = keep.tile([P, BIAS_ROWS, P], F32, name="bias")
+        nc.vector.tensor_copy(out=bias[:], in_=spread_ps[:, 0:BIAS_ROWS, :])
+
+        ctx_codes = []
+        ctx_scales = []
+        for b in range(B):
+            grouped = keep.tile([P, PASSES, S, PACK], BF16, name="ctx_grouped%d" % b, align_bytes=64)
+            for g in range(PASSES):
+                c_ps = psum_c.tile([P, PACK, S], F32, name="c_ps")
+                for t in range(PACK):
+                    h = g * PACK + t
+                    nc.tensor.matmul(
+                        c_ps[:, t, :],
+                        lhsT=kv_sb[b][:, h, :],
+                        rhs=q_t[b][:, h, :, :].rearrange("d j u -> d (j u)"),
+                        start=True,
+                        stop=True,
+                    )
+                first = b * H + g * PACK
+                nc.vector.tensor_tensor(
+                    out=grouped[:, g, :, :].rearrange("p (u j) t -> p u j t", j=ROWS),
+                    in0=c_ps[:].rearrange("p t (j u) -> p u j t", u=RUNS),
+                    in1=recip[:, first : first + PACK].unsqueeze(1).unsqueeze(1).to_broadcast([P, RUNS, ROWS, PACK]),
+                    op=MULT,
+                )
+            codes = keep.tile([P, PASSES * S], U32, name="ctx_codes%d" % b, align_bytes=64)
+            scales = keep.tile([P, PASSES * S], U8, name="ctx_scales%d" % b, align_bytes=64)
+            nc.vector.quantize_mx(
+                out=codes[:].bitcast(FP8X4),
+                scales=scales[:],
+                in_=grouped[:].rearrange("p g s t -> p (g s t)"),
+            )
+            ctx_codes.append(codes)
+            ctx_scales.append(scales)
+
+        wo_codes = []
+        wo_scales = []
+        for g in range(PASSES):
+            grouped = keep.tile([P, E, PACK], BF16, name="wo_grouped%d" % g, align_bytes=64)
+            dst = grouped[:].rearrange("p (c i) t -> p c t i", i=4)
+            src = wo_raw[g][:].rearrange("p t (c i) -> p c t i", i=4)
+            cut = VECTOR_COLS // 4
+            nc.vector.tensor_copy(out=dst[:, 0:cut], in_=src[:, 0:cut])
+            nc.scalar.copy(out=dst[:, cut:], in_=src[:, cut:])
+            codes = keep.tile([P, E], U32, name="wo_codes%d" % g, align_bytes=64)
+            scales = keep.tile([P, E], U8, name="wo_scales%d" % g, align_bytes=64)
+            nc.vector.quantize_mx(
+                out=codes[:].bitcast(FP8X4),
+                scales=scales[:],
+                in_=grouped[:].rearrange("p n t -> p (n t)"),
+            )
+            wo_codes.append(codes)
+            wo_scales.append(scales)
+
+        o_ps = [psum_o.tile([P, E], F32, name="o_ps") for b in range(B)]
+        for g in range(PASSES):
+            for b in range(B):
+                nc.tensor.matmul_mx(
+                    out=o_ps[b][:],
+                    lhsT=ctx_codes[b][:, g * S : (g + 1) * S].bitcast(FP8X4),
+                    lhsT_scale=ctx_scales[b][:, g * S : (g + 1) * S],
+                    rhs=wo_codes[g][:].bitcast(FP8X4),
+                    rhs_scale=wo_scales[g][:],
+                    start=(g == 0),
+                    stop=(g == PASSES - 1),
+                )
+        for b in range(B):
+            result = keep.tile([P, E], F32, name="result%d" % b)
+            nc.vector.tensor_tensor(
+                out=result[:], in0=o_ps[b][:], in1=bias[:].rearrange("p c n -> p (c n)"), op=ADD
+            )
+            nc.sync.dma_start(out=out[b], in_=result[:])

@@ -19,11 +19,9 @@ DH = 128
 E = 512
 PACK = 4
 PASSES = H // PACK
-ROWS = 8
+ROWS = 4
 RUNS = S // ROWS
-HALF = ROWS // 2
-BIAS_ROWS = E // P
-VECTOR_COLS = 256
+VECTOR_COLS = 192
 
 FLOPS = 2 * B * H * S * DH * DH + 2 * B * S * H * DH * E
 
@@ -35,16 +33,25 @@ def tile_linearattention_pb_s_kernel(tc, q_feat, kv, denom, Wo, bo, out):
         psum_t = ctx.enter_context(tc.psum_pool(name="psum_t", bufs=2))
         psum_c = ctx.enter_context(tc.psum_pool(name="psum_c", bufs=4))
         psum_o = ctx.enter_context(tc.psum_pool(name="psum_o", bufs=2))
+        ctx.enter_context(tc.manual_schedule())
 
+        denom_all = keep.tile([P, B * H], BF16, name="denom_all")
+        nc.sync.dma_start(out=denom_all[:], in_=denom.rearrange("b h x y -> (b h x y)").partition_broadcast(P))
+        bias_row = keep.tile([P, E], BF16, name="bias_row")
+        nc.vector.memset(bias_row[:], 0.0)
+        nc.sync.dma_start(out=bias_row[0:1, :], in_=bo.unsqueeze(0))
         q_rows = []
-        for b in range(B):
-            q_b = keep.tile([P, ROWS, DH], BF16, name="q_rows%d" % b)
-            nc.sync.dma_start(out=q_b[:], in_=q_feat[b].rearrange("h (u j) d -> (h u) j d", j=ROWS))
-            q_rows.append(q_b)
         kv_sb = []
         for b in range(B):
+            q_b = keep.tile([P, PASSES, ROWS, DH], BF16, name="q_rows%d" % b)
+            nc.sync.dma_start(
+                out=q_b[:], in_=q_feat[b].rearrange("(g t) (u j) d -> (t u) g j d", t=PACK, j=ROWS)
+            )
+            q_rows.append(q_b)
             kv_b = keep.tile([P, H, DH], BF16, name="kv_sb%d" % b)
-            nc.sync.dma_start(out=kv_b[:], in_=kv[b].rearrange("h d e -> d h e"))
+            for g in range(PASSES):
+                heads = slice(g * PACK, (g + 1) * PACK)
+                nc.sync.dma_start(out=kv_b[:, heads, :], in_=kv[b, heads].rearrange("h d e -> d h e"))
             kv_sb.append(kv_b)
         wo_view = Wo.rearrange("(g t p) n -> g p t n", t=PACK, p=P)
         wo_raw = []
@@ -53,110 +60,98 @@ def tile_linearattention_pb_s_kernel(tc, q_feat, kv, denom, Wo, bo, out):
             nc.sync.dma_start(out=wo_g[:], in_=wo_view[g])
             wo_raw.append(wo_g)
 
-        vec_rows = keep.tile([P, P], BF16, name="vec_rows")
-        nc.vector.memset(vec_rows[:], 0.0)
-        nc.scalar.dma_start(out=vec_rows[0:BIAS_ROWS, :], in_=bo.rearrange("(c n) -> c n", c=BIAS_ROWS))
-        nc.scalar.dma_start(
-            out=vec_rows[BIAS_ROWS : BIAS_ROWS + 1, 0 : B * H],
-            in_=denom.rearrange("b h x y -> (x y) (b h)"),
-        )
-
         ident = keep.tile([P, P], BF16, name="ident")
         make_identity(nc, ident[:])
+        ones = keep.tile([P, P], BF16, name="ones")
+        nc.vector.memset(ones[:], 1.0)
 
-        q_t = []
-        for b in range(B):
-            q_t_b = keep.tile([P, H, ROWS, RUNS], BF16, name="q_t%d" % b)
-            for half in range(2):
-                t_ps = psum_t.tile([P, HALF, P], BF16, name="t_ps")
-                for jj in range(HALF):
-                    nc.tensor.transpose(t_ps[:, jj, :], q_rows[b][:, half * HALF + jj, :], ident[:])
-                sorted_view = t_ps[:].rearrange("d j (h u) -> d h j u", u=RUNS)
-                target = q_t_b[:, :, half * HALF : (half + 1) * HALF, :]
-                if half == 0:
-                    nc.vector.tensor_copy(out=target, in_=sorted_view)
-                else:
-                    nc.scalar.copy(out=target, in_=sorted_view)
-            q_t.append(q_t_b)
-
-        cols_ps = psum_o.tile([P, P], BF16, name="o_ps")
-        nc.tensor.transpose(cols_ps[:], vec_rows[:], ident[:])
-        vec_cols = keep.tile([P, BIAS_ROWS + 1], BF16, name="vec_cols")
-        nc.vector.tensor_copy(out=vec_cols[:], in_=cols_ps[:, 0 : BIAS_ROWS + 1])
-        spread_ps = psum_o.tile([P, BIAS_ROWS + 1, P], BF16, name="o_ps")
-        for c in range(BIAS_ROWS + 1):
-            nc.tensor.transpose(spread_ps[:, c, :], vec_cols[:, c : c + 1].to_broadcast([P, P]), ident[:])
         recip = keep.tile([P, B * H], F32, name="recip")
-        nc.vector.reciprocal(out=recip[:], in_=spread_ps[:, BIAS_ROWS, 0 : B * H])
-        bias = keep.tile([P, BIAS_ROWS, P], F32, name="bias")
-        nc.vector.tensor_copy(out=bias[:], in_=spread_ps[:, 0:BIAS_ROWS, :])
+        nc.vector.reciprocal(out=recip[:], in_=denom_all[:])
 
-        ctx_codes = []
-        ctx_scales = []
-        for b in range(B):
-            grouped = keep.tile([P, PASSES, S, PACK], BF16, name="ctx_grouped%d" % b, align_bytes=64)
-            for g in range(PASSES):
-                c_ps = psum_c.tile([P, PACK, S], F32, name="c_ps")
-                for t in range(PACK):
-                    h = g * PACK + t
-                    nc.tensor.matmul(
-                        c_ps[:, t, :],
-                        lhsT=kv_sb[b][:, h, :],
-                        rhs=q_t[b][:, h, :, :].rearrange("d j u -> d (j u)"),
-                        start=True,
-                        stop=True,
-                    )
-                first = b * H + g * PACK
-                nc.vector.tensor_tensor(
-                    out=grouped[:, g, :, :].rearrange("p (u j) t -> p u j t", j=ROWS),
-                    in0=c_ps[:].rearrange("p t (j u) -> p u j t", u=RUNS),
-                    in1=recip[:, first : first + PACK].unsqueeze(1).unsqueeze(1).to_broadcast([P, RUNS, ROWS, PACK]),
-                    op=MULT,
+        bias_ps = psum_o.tile([P, E], F32, name="o_ps")
+        nc.tensor.matmul(bias_ps[:], lhsT=ones[:], rhs=bias_row[:], start=True, stop=True)
+        bias = keep.tile([P, E], F32, name="bias")
+        nc.scalar.copy(out=bias[:], in_=bias_ps[:])
+
+        def transpose_q(b, g):
+            t_ps = psum_t.tile([P, ROWS, P], BF16, name="t_ps")
+            for j in range(ROWS):
+                nc.tensor.transpose(t_ps[:, j, :], q_rows[b][:, g, j, :], ident[:])
+            q_t = keep.tile([P, PACK, ROWS, RUNS], BF16, name="q_t%d%d" % (b, g))
+            nc.scalar.copy(out=q_t[:], in_=t_ps[:].rearrange("d j (t u) -> d t j u", u=RUNS))
+            return q_t
+
+        ctx_grouped = [
+            keep.tile([P, PASSES, S, PACK], BF16, name="ctx_grouped%d" % b, align_bytes=64) for b in range(B)
+        ]
+
+        def first_matmul(b, g, q_t):
+            c_ps = psum_c.tile([P, PACK, S], F32, name="c_ps")
+            for t in range(PACK):
+                nc.tensor.matmul(
+                    c_ps[:, t, :],
+                    lhsT=kv_sb[b][:, g * PACK + t, :],
+                    rhs=q_t[:, t, :, :].rearrange("d j u -> d (j u)"),
+                    start=True,
+                    stop=True,
                 )
-            codes = keep.tile([P, PASSES * S], U32, name="ctx_codes%d" % b, align_bytes=64)
-            scales = keep.tile([P, PASSES * S], U8, name="ctx_scales%d" % b, align_bytes=64)
-            nc.vector.quantize_mx(
-                out=codes[:].bitcast(FP8X4),
-                scales=scales[:],
-                in_=grouped[:].rearrange("p g s t -> p (g s t)"),
+            first = b * H + g * PACK
+            nc.vector.tensor_tensor(
+                out=ctx_grouped[b][:, g, :, :].rearrange("p (u j) t -> p u j t", j=ROWS),
+                in0=c_ps[:].rearrange("p t (j u) -> p u j t", u=RUNS),
+                in1=recip[:, first : first + PACK].unsqueeze(1).unsqueeze(1).to_broadcast([P, RUNS, ROWS, PACK]),
+                op=MULT,
             )
-            ctx_codes.append(codes)
-            ctx_scales.append(scales)
 
-        wo_codes = []
-        wo_scales = []
-        for g in range(PASSES):
-            grouped = keep.tile([P, E, PACK], BF16, name="wo_grouped%d" % g, align_bytes=64)
-            dst = grouped[:].rearrange("p (c i) t -> p c t i", i=4)
+        def quantise(grouped_flat, width, name):
+            codes = keep.tile([P, width], U32, name=name + "_codes", align_bytes=64)
+            scales = keep.tile([P, width], U8, name=name + "_scales", align_bytes=64)
+            nc.vector.quantize_mx(out=codes[:].bitcast(FP8X4), scales=scales[:], in_=grouped_flat)
+            return codes, scales
+
+        def quantise_ctx(b):
+            return quantise(ctx_grouped[b][:].rearrange("p g s t -> p (g s t)"), PASSES * S, "ctx%d" % b)
+
+        wo_grouped = [keep.tile([P, E, PACK], BF16, name="wo_grouped%d" % g, align_bytes=64) for g in range(PASSES)]
+
+        def regroup_wo(g):
+            dst = wo_grouped[g][:].rearrange("p (c i) t -> p c t i", i=4)
             src = wo_raw[g][:].rearrange("p t (c i) -> p c t i", i=4)
             cut = VECTOR_COLS // 4
             nc.vector.tensor_copy(out=dst[:, 0:cut], in_=src[:, 0:cut])
             nc.scalar.copy(out=dst[:, cut:], in_=src[:, cut:])
-            codes = keep.tile([P, E], U32, name="wo_codes%d" % g, align_bytes=64)
-            scales = keep.tile([P, E], U8, name="wo_scales%d" % g, align_bytes=64)
-            nc.vector.quantize_mx(
-                out=codes[:].bitcast(FP8X4),
-                scales=scales[:],
-                in_=grouped[:].rearrange("p n t -> p (n t)"),
-            )
-            wo_codes.append(codes)
-            wo_scales.append(scales)
+
+        def quantise_wo(g):
+            return quantise(wo_grouped[g][:].rearrange("p n t -> p (n t)"), E, "wo%d" % g)
+
+        q_t00 = transpose_q(0, 0)
+        q_t01 = transpose_q(0, 1)
+        first_matmul(0, 0, q_t00)
+        first_matmul(0, 1, q_t01)
+        q_t10 = transpose_q(1, 0)
+        q_t11 = transpose_q(1, 1)
+        first_matmul(1, 0, q_t10)
+        ctx_mx = [quantise_ctx(0)]
+        first_matmul(1, 1, q_t11)
+        regroup_wo(0)
+        ctx_mx.append(quantise_ctx(1))
+        wo_mx = [quantise_wo(0)]
+        regroup_wo(1)
+        wo_mx.append(quantise_wo(1))
 
         o_ps = [psum_o.tile([P, E], F32, name="o_ps") for b in range(B)]
         for g in range(PASSES):
             for b in range(B):
                 nc.tensor.matmul_mx(
                     out=o_ps[b][:],
-                    lhsT=ctx_codes[b][:, g * S : (g + 1) * S].bitcast(FP8X4),
-                    lhsT_scale=ctx_scales[b][:, g * S : (g + 1) * S],
-                    rhs=wo_codes[g][:].bitcast(FP8X4),
-                    rhs_scale=wo_scales[g][:],
+                    lhsT=ctx_mx[b][0][:, g * S : (g + 1) * S].bitcast(FP8X4),
+                    lhsT_scale=ctx_mx[b][1][:, g * S : (g + 1) * S],
+                    rhs=wo_mx[g][0][:].bitcast(FP8X4),
+                    rhs_scale=wo_mx[g][1][:],
                     start=(g == 0),
                     stop=(g == PASSES - 1),
                 )
         for b in range(B):
             result = keep.tile([P, E], F32, name="result%d" % b)
-            nc.vector.tensor_tensor(
-                out=result[:], in0=o_ps[b][:], in1=bias[:].rearrange("p c n -> p (c n)"), op=ADD
-            )
+            nc.vector.tensor_tensor(out=result[:], in0=o_ps[b][:], in1=bias[:], op=ADD)
             nc.sync.dma_start(out=out[b], in_=result[:])

@@ -36,18 +36,19 @@ def tile_linearattention_pb_s_kernel(tc, q_feat, kv, denom, Wo, bo, out):
         ctx.enter_context(tc.manual_schedule())
 
         denom_all = keep.tile([P, B * H], BF16, name="denom_all")
-        nc.sync.dma_start(out=denom_all[:], in_=denom.rearrange("b h x y -> (b h x y)").partition_broadcast(P))
+        nc.scalar.dma_start(out=denom_all[:], in_=denom.rearrange("b h x y -> (b h x y)").partition_broadcast(P))
         bias_row = keep.tile([P, E], BF16, name="bias_row")
         nc.vector.memset(bias_row[:], 0.0)
         nc.sync.dma_start(out=bias_row[0:1, :], in_=bo.unsqueeze(0))
         q_rows = []
-        kv_sb = []
         for b in range(B):
             q_b = keep.tile([P, PASSES, ROWS, DH], BF16, name="q_rows%d" % b)
             nc.sync.dma_start(
                 out=q_b[:], in_=q_feat[b].rearrange("(g t) (u j) d -> (t u) g j d", t=PACK, j=ROWS)
             )
             q_rows.append(q_b)
+        kv_sb = []
+        for b in range(B):
             kv_b = keep.tile([P, H, DH], BF16, name="kv_sb%d" % b)
             for g in range(PASSES):
                 heads = slice(g * PACK, (g + 1) * PACK)
@@ -65,20 +66,23 @@ def tile_linearattention_pb_s_kernel(tc, q_feat, kv, denom, Wo, bo, out):
         ones = keep.tile([P, P], BF16, name="ones")
         nc.vector.memset(ones[:], 1.0)
 
-        recip = keep.tile([P, B * H], F32, name="recip")
-        nc.vector.reciprocal(out=recip[:], in_=denom_all[:])
-
         bias_ps = psum_o.tile([P, E], F32, name="o_ps")
         nc.tensor.matmul(bias_ps[:], lhsT=ones[:], rhs=bias_row[:], start=True, stop=True)
         bias = keep.tile([P, E], F32, name="bias")
         nc.scalar.copy(out=bias[:], in_=bias_ps[:])
+
+        recip = keep.tile([P, B * H], F32, name="recip")
 
         def transpose_q(b, g):
             t_ps = psum_t.tile([P, ROWS, P], BF16, name="t_ps")
             for j in range(ROWS):
                 nc.tensor.transpose(t_ps[:, j, :], q_rows[b][:, g, j, :], ident[:])
             q_t = keep.tile([P, PACK, ROWS, RUNS], BF16, name="q_t%d%d" % (b, g))
-            nc.scalar.copy(out=q_t[:], in_=t_ps[:].rearrange("d j (t u) -> d t j u", u=RUNS))
+            sorted_view = t_ps[:].rearrange("d j (t u) -> d t j u", u=RUNS)
+            if g == 0:
+                nc.scalar.copy(out=q_t[:], in_=sorted_view)
+            else:
+                nc.vector.tensor_copy(out=q_t[:], in_=sorted_view)
             return q_t
 
         ctx_grouped = [
@@ -124,15 +128,13 @@ def tile_linearattention_pb_s_kernel(tc, q_feat, kv, denom, Wo, bo, out):
         def quantise_wo(g):
             return quantise(wo_grouped[g][:].rearrange("p n t -> p (n t)"), E, "wo%d" % g)
 
-        q_t00 = transpose_q(0, 0)
-        q_t01 = transpose_q(0, 1)
-        first_matmul(0, 0, q_t00)
-        first_matmul(0, 1, q_t01)
-        q_t10 = transpose_q(1, 0)
-        q_t11 = transpose_q(1, 1)
-        first_matmul(1, 0, q_t10)
+        q_ts = [[transpose_q(b, g) for g in range(PASSES)] for b in range(B)]
+        nc.vector.reciprocal(out=recip[:], in_=denom_all[:])
+        first_matmul(0, 0, q_ts[0][0])
+        first_matmul(0, 1, q_ts[0][1])
+        first_matmul(1, 0, q_ts[1][0])
         ctx_mx = [quantise_ctx(0)]
-        first_matmul(1, 1, q_t11)
+        first_matmul(1, 1, q_ts[1][1])
         regroup_wo(0)
         ctx_mx.append(quantise_ctx(1))
         wo_mx = [quantise_wo(0)]

@@ -21,7 +21,7 @@ PACK = 4
 PASSES = H // PACK
 ROWS = 4
 RUNS = S // ROWS
-VECTOR_COLS = 192
+VECTOR_COLS = 256
 
 FLOPS = 2 * B * H * S * DH * DH + 2 * B * S * H * DH * E
 
@@ -35,54 +35,54 @@ def tile_linearattention_pb_s_kernel(tc, q_feat, kv, denom, Wo, bo, out):
         psum_o = ctx.enter_context(tc.psum_pool(name="psum_o", bufs=2))
         ctx.enter_context(tc.manual_schedule())
 
-        denom_all = keep.tile([P, B * H], BF16, name="denom_all")
-        nc.scalar.dma_start(out=denom_all[:], in_=denom.rearrange("b h x y -> (b h x y)").partition_broadcast(P))
         bias_row = keep.tile([P, E], BF16, name="bias_row")
+        denom_all = keep.tile([P, B * H], BF16, name="denom_all")
+        q_rows = [keep.tile([P, PASSES, ROWS, DH], BF16, name="q_rows%d" % b) for b in range(B)]
+        kv_sb = [keep.tile([P, H, DH], BF16, name="kv_sb%d" % b) for b in range(B)]
+        wo_raw = [keep.tile([P, PACK, E], BF16, name="wo_raw%d" % g) for g in range(PASSES)]
+
+        def load_q(b):
+            nc.sync.dma_start(
+                out=q_rows[b][:], in_=q_feat[b].rearrange("(g t) (u j) d -> (t u) g j d", t=PACK, j=ROWS)
+            )
+
+        def load_kv(b, g):
+            heads = slice(g * PACK, (g + 1) * PACK)
+            nc.sync.dma_start(out=kv_sb[b][:, heads, :], in_=kv[b, heads].rearrange("h d e -> d h e"))
+
+        def load_wo(g):
+            nc.sync.dma_start(out=wo_raw[g][:], in_=Wo.rearrange("(g t p) n -> g p t n", t=PACK, p=P)[g])
+
         nc.vector.memset(bias_row[:], 0.0)
         nc.sync.dma_start(out=bias_row[0:1, :], in_=bo.unsqueeze(0))
-        q_rows = []
-        for b in range(B):
-            q_b = keep.tile([P, PASSES, ROWS, DH], BF16, name="q_rows%d" % b)
-            nc.sync.dma_start(
-                out=q_b[:], in_=q_feat[b].rearrange("(g t) (u j) d -> (t u) g j d", t=PACK, j=ROWS)
-            )
-            q_rows.append(q_b)
-        kv_sb = []
-        for b in range(B):
-            kv_b = keep.tile([P, H, DH], BF16, name="kv_sb%d" % b)
-            for g in range(PASSES):
-                heads = slice(g * PACK, (g + 1) * PACK)
-                nc.sync.dma_start(out=kv_b[:, heads, :], in_=kv[b, heads].rearrange("h d e -> d h e"))
-            kv_sb.append(kv_b)
-        wo_view = Wo.rearrange("(g t p) n -> g p t n", t=PACK, p=P)
-        wo_raw = []
-        for g in range(PASSES):
-            wo_g = keep.tile([P, PACK, E], BF16, name="wo_raw%d" % g)
-            nc.sync.dma_start(out=wo_g[:], in_=wo_view[g])
-            wo_raw.append(wo_g)
+        load_q(0)
+        nc.sync.dma_start(out=denom_all[:], in_=denom.rearrange("b h x y -> (b h x y)").partition_broadcast(P))
+        load_kv(0, 0)
+        load_kv(0, 1)
+        load_q(1)
+        load_kv(1, 0)
+        load_kv(1, 1)
+        load_wo(0)
+        load_wo(1)
 
         ident = keep.tile([P, P], BF16, name="ident")
         make_identity(nc, ident[:])
         ones = keep.tile([P, P], BF16, name="ones")
         nc.vector.memset(ones[:], 1.0)
 
+        recip = keep.tile([P, B * H], F32, name="recip")
+        nc.vector.reciprocal(out=recip[:], in_=denom_all[:])
+
         bias_ps = psum_o.tile([P, E], F32, name="o_ps")
         nc.tensor.matmul(bias_ps[:], lhsT=ones[:], rhs=bias_row[:], start=True, stop=True)
         bias = keep.tile([P, E], F32, name="bias")
-        nc.scalar.copy(out=bias[:], in_=bias_ps[:])
-
-        recip = keep.tile([P, B * H], F32, name="recip")
 
         def transpose_q(b, g):
             t_ps = psum_t.tile([P, ROWS, P], BF16, name="t_ps")
             for j in range(ROWS):
                 nc.tensor.transpose(t_ps[:, j, :], q_rows[b][:, g, j, :], ident[:])
             q_t = keep.tile([P, PACK, ROWS, RUNS], BF16, name="q_t%d%d" % (b, g))
-            sorted_view = t_ps[:].rearrange("d j (t u) -> d t j u", u=RUNS)
-            if g == 0:
-                nc.scalar.copy(out=q_t[:], in_=sorted_view)
-            else:
-                nc.vector.tensor_copy(out=q_t[:], in_=sorted_view)
+            nc.scalar.copy(out=q_t[:], in_=t_ps[:].rearrange("d j (t u) -> d t j u", u=RUNS))
             return q_t
 
         ctx_grouped = [
@@ -128,13 +128,16 @@ def tile_linearattention_pb_s_kernel(tc, q_feat, kv, denom, Wo, bo, out):
         def quantise_wo(g):
             return quantise(wo_grouped[g][:].rearrange("p n t -> p (n t)"), E, "wo%d" % g)
 
-        q_ts = [[transpose_q(b, g) for g in range(PASSES)] for b in range(B)]
-        nc.vector.reciprocal(out=recip[:], in_=denom_all[:])
-        first_matmul(0, 0, q_ts[0][0])
-        first_matmul(0, 1, q_ts[0][1])
-        first_matmul(1, 0, q_ts[1][0])
+        q_t00 = transpose_q(0, 0)
+        q_t01 = transpose_q(0, 1)
+        first_matmul(0, 0, q_t00)
+        first_matmul(0, 1, q_t01)
+        nc.scalar.copy(out=bias[:], in_=bias_ps[:])
         ctx_mx = [quantise_ctx(0)]
-        first_matmul(1, 1, q_ts[1][1])
+        q_t10 = transpose_q(1, 0)
+        q_t11 = transpose_q(1, 1)
+        first_matmul(1, 0, q_t10)
+        first_matmul(1, 1, q_t11)
         regroup_wo(0)
         ctx_mx.append(quantise_ctx(1))
         wo_mx = [quantise_wo(0)]

from contextlib import ExitStack

import concourse.mybir as mybir
from concourse.masks import make_identity

BF16 = mybir.dt.bfloat16
F32 = mybir.dt.float32
U32 = mybir.dt.uint32
U8 = mybir.dt.uint8
FP8X4 = mybir.dt.float8_e4m3fn_x4
MULT = mybir.AluOpType.mult
ADD = mybir.AluOpType.add

P = 128
B = 2
H = 8
S = 128
DH = 128
E = 512
PACK = 4
PASSES = H // PACK
ROWS = 4
RUNS = S // ROWS
VECTOR_COLS = 256

FLOPS = 2 * B * H * S * DH * DH + 2 * B * S * H * DH * E


def tile_linearattention_pb_s_kernel(tc, q_feat, kv, denom, Wo, bo, out):
    nc = tc.nc
    with ExitStack() as ctx:
        keep = ctx.enter_context(tc.tile_pool(name="keep", bufs=1))
        psum_t = ctx.enter_context(tc.psum_pool(name="psum_t", bufs=2))
        psum_c = ctx.enter_context(tc.psum_pool(name="psum_c", bufs=4))
        psum_o = ctx.enter_context(tc.psum_pool(name="psum_o", bufs=2))
        ctx.enter_context(tc.manual_schedule())

        bias_row = keep.tile([P, E], BF16, name="bias_row")
        denom_all = keep.tile([P, B * H], BF16, name="denom_all")
        q_rows = [keep.tile([P, PASSES, ROWS, DH], BF16, name="q_rows%d" % b) for b in range(B)]
        kv_sb = [keep.tile([P, H, DH], BF16, name="kv_sb%d" % b) for b in range(B)]
        wo_raw = [keep.tile([P, PACK, E], BF16, name="wo_raw%d" % g) for g in range(PASSES)]

        def load_q(b):
            nc.sync.dma_start(
                out=q_rows[b][:], in_=q_feat[b].rearrange("(g t) (u j) d -> (t u) g j d", t=PACK, j=ROWS)
            )

        def load_kv(b, g):
            heads = slice(g * PACK, (g + 1) * PACK)
            nc.sync.dma_start(out=kv_sb[b][:, heads, :], in_=kv[b, heads].rearrange("h d e -> d h e"))

        def load_wo(g):
            nc.sync.dma_start(out=wo_raw[g][:], in_=Wo.rearrange("(g t p) n -> g p t n", t=PACK, p=P)[g])

        nc.vector.memset(bias_row[:], 0.0)
        nc.sync.dma_start(out=bias_row[0:1, :], in_=bo.unsqueeze(0))
        load_q(0)
        nc.sync.dma_start(out=denom_all[:], in_=denom.rearrange("b h x y -> (b h x y)").partition_broadcast(P))
        load_kv(0, 0)
        load_kv(0, 1)
        load_q(1)
        load_kv(1, 0)
        load_kv(1, 1)
        load_wo(0)
        load_wo(1)

        ident = keep.tile([P, P], BF16, name="ident")
        make_identity(nc, ident[:])
        ones = keep.tile([P, P], BF16, name="ones")
        nc.vector.memset(ones[:], 1.0)

        recip = keep.tile([P, B * H], F32, name="recip")
        nc.vector.reciprocal(out=recip[:], in_=denom_all[:])

        bias_ps = psum_o.tile([P, E], F32, name="o_ps")
        nc.tensor.matmul(bias_ps[:], lhsT=ones[:], rhs=bias_row[:], start=True, stop=True)
        bias = keep.tile([P, E], F32, name="bias")

        def transpose_q(b, g):
            t_ps = psum_t.tile([P, ROWS, P], BF16, name="t_ps")
            for j in range(ROWS):
                nc.tensor.transpose(t_ps[:, j, :], q_rows[b][:, g, j, :], ident[:])
            q_t = keep.tile([P, PACK, ROWS, RUNS], BF16, name="q_t%d%d" % (b, g))
            nc.scalar.copy(out=q_t[:], in_=t_ps[:].rearrange("d j (t u) -> d t j u", u=RUNS))
            return q_t

        ctx_grouped = [
            keep.tile([P, PASSES, S, PACK], BF16, name="ctx_grouped%d" % b, align_bytes=64) for b in range(B)
        ]

        def first_matmul(b, g, q_t):
            c_ps = psum_c.tile([P, PACK, S], F32, name="c_ps")
            for t in range(PACK):
                nc.tensor.matmul(
                    c_ps[:, t, :],
                    lhsT=kv_sb[b][:, g * PACK + t, :],
                    rhs=q_t[:, t, :, :].rearrange("d j u -> d (j u)"),
                    start=True,
                    stop=True,
                )
            first = b * H + g * PACK
            nc.vector.tensor_tensor(
                out=ctx_grouped[b][:, g, :, :].rearrange("p (u j) t -> p u j t", j=ROWS),
                in0=c_ps[:].rearrange("p t (j u) -> p u j t", u=RUNS),
                in1=recip[:, first : first + PACK].unsqueeze(1).unsqueeze(1).to_broadcast([P, RUNS, ROWS, PACK]),
                op=MULT,
            )

        def quantise(grouped_flat, width, name):
            codes = keep.tile([P, width], U32, name=name + "_codes", align_bytes=64)
            scales = keep.tile([P, width], U8, name=name + "_scales", align_bytes=64)
            nc.vector.quantize_mx(out=codes[:].bitcast(FP8X4), scales=scales[:], in_=grouped_flat)
            return codes, scales

        def quantise_ctx(b):
            return quantise(ctx_grouped[b][:].rearrange("p g s t -> p (g s t)"), PASSES * S, "ctx%d" % b)

        wo_grouped = [keep.tile([P, E, PACK], BF16, name="wo_grouped%d" % g, align_bytes=64) for g in range(PASSES)]

        def regroup_wo(g):
            dst = wo_grouped[g][:].rearrange("p (c i) t -> p c t i", i=4)
            src = wo_raw[g][:].rearrange("p t (c i) -> p c t i", i=4)
            cut = VECTOR_COLS // 4
            nc.vector.tensor_copy(out=dst[:, 0:cut], in_=src[:, 0:cut])
            nc.scalar.copy(out=dst[:, cut:], in_=src[:, cut:])

        def quantise_wo(g):
            return quantise(wo_grouped[g][:].rearrange("p n t -> p (n t)"), E, "wo%d" % g)

        q_t00 = transpose_q(0, 0)
        q_t01 = transpose_q(0, 1)
        first_matmul(0, 0, q_t00)
        first_matmul(0, 1, q_t01)
        nc.scalar.copy(out=bias[:], in_=bias_ps[:])
        ctx_mx = [quantise_ctx(0)]
        q_t10 = transpose_q(1, 0)
        q_t11 = transpose_q(1, 1)
        first_matmul(1, 0, q_t10)
        first_matmul(1, 1, q_t11)
        regroup_wo(0)
        ctx_mx.append(quantise_ctx(1))
        wo_mx = [quantise_wo(0)]
        regroup_wo(1)
        wo_mx.append(quantise_wo(1))

        o_ps = [psum_o.tile([P, E], F32, name="o_ps") for b in range(B)]
        for g in range(PASSES):
            for b in range(B):
                nc.tensor.matmul_mx(
                    out=o_ps[b][:],
                    lhsT=ctx_mx[b][0][:, g * S : (g + 1) * S].bitcast(FP8X4),
                    lhsT_scale=ctx_mx[b][1][:, g * S : (g + 1) * S],
                    rhs=wo_mx[g][0][:].bitcast(FP8X4),
                    rhs_scale=wo_mx[g][1][:],
                    start=(g == 0),
                    stop=(g == PASSES - 1),
                )
        for b in range(B):
            result = keep.tile([P, E], F32, name="result%d" % b)
            nc.vector.tensor_tensor(out=result[:], in0=o_ps[b][:], in1=bias[:], op=ADD)
            nc.sync.dma_start(out=out[b], in_=result[:])
